import numpy as np
import ml_dtypes


def mxq(x, axis, fmt="e4m3"):
    dtype, down = {"e4m3": (ml_dtypes.float8_e4m3fn, 7), "e5m2": (ml_dtypes.float8_e5m2, 14)}[fmt]
    v = np.moveaxis(np.asarray(x, np.float32).astype(ml_dtypes.bfloat16).astype(np.float64), axis, -1)
    blocks = v.reshape(v.shape[:-1] + (-1, 32))
    amax = np.abs(blocks).max(-1, keepdims=True)
    byte = np.maximum(np.where(amax > 0, np.frexp(amax)[1] - 1 + 127, 0) - down, 1)
    scale = np.exp2(byte - 127.0)
    codes = (blocks / scale).astype(np.float32).astype(dtype).astype(np.float64)
    return np.moveaxis((codes * scale).reshape(v.shape), -1, axis)


WIDE = False


def mx_kscale(k):
    if not WIDE:
        return np.ones(k)
    levels = np.array([10, -10, 5, -5, 0])
    a = np.random.permutation(np.resize(levels, k // 512 * 4)).reshape(k // 512, 4)
    idx = np.arange(k)
    return np.exp2(a[idx // 512, idx % 128 // 32])


BF16 = ml_dtypes.bfloat16


def bf(x):
    return np.asarray(x, np.float32).astype(BF16)


def f64(x):
    return np.asarray(x).astype(np.float64)


B, N, D_IN, D_H, NM = 4, 512, 256, 256, 5


def setup_inputs():
    s = mx_kscale(N)
    sup = s[:, None] / s[None, :] * 0.7 / np.sqrt(N)
    return {"x": bf(np.random.standard_normal((B, N, D_IN)) * s[None, :, None]),
            "h": bf(np.random.standard_normal((B, N, D_H)) * s[None, :, None]),
            "support0": bf(np.random.standard_normal((N, N)) * sup),
            "support1": bf(np.random.standard_normal((N, N)) * sup)}


def reference(x, h, support0, support1):
    x0 = np.concatenate([f64(x), f64(h)], axis=-1)
    x0q = mxq(x0, 1, "e4m3")
    stack = [x0]
    for sup in (support0, support1):
        sq = mxq(f64(sup), 1, "e4m3")
        x1 = sq @ x0q
        x2 = 2.0 * (sq @ mxq(x1, 1, "e4m3")) - x0
        stack += [x1, x2]
    return np.concatenate(stack, axis=-1)

@@ -1,0 +1,222 @@
+from contextlib import ExitStack
+
+import concourse.mybir as mybir
+from concourse.masks import make_identity
+
+F32 = mybir.dt.float32
+BF16 = mybir.dt.bfloat16
+U32 = mybir.dt.uint32
+U8 = mybir.dt.uint8
+FP8X4 = mybir.dt.float8_e4m3fn_x4
+MULT = mybir.AluOpType.mult
+SUBTRACT = mybir.AluOpType.subtract
+
+P = 128
+PACK = 4
+BATCH = 4
+NODES = 512
+HALF = 256
+FEAT = 512
+NSUP = 2
+UNITS = BATCH * NSUP
+CHUNK = 128
+OUT_COLS = 2560
+
+FLOPS = 2 * NSUP * 2 * BATCH * NODES * NODES * FEAT
+
+MANUAL = True
+
+
+def tile_dcgrucell_pa_kernel(tc, x, h, support0, support1, out):
+    nc = tc.nc
+    supports = (support0, support1)
+    with ExitStack() as ctx:
+        if MANUAL:
+            ctx.enter_context(tc.manual_schedule())
+        keep = ctx.enter_context(tc.tile_pool(name="keep", bufs=1))
+        g0_pool = ctx.enter_context(tc.tile_pool(name="g0p", bufs=2))
+        g1_pool = ctx.enter_context(tc.tile_pool(name="g1p", bufs=3))
+        st0_pool = ctx.enter_context(tc.tile_pool(name="st0p", bufs=4))
+        st_pool = ctx.enter_context(tc.tile_pool(name="stp", bufs=6))
+        ps_a = ctx.enter_context(tc.psum_pool(name="psa", bufs=4))
+        ps_b = ctx.enter_context(tc.psum_pool(name="psb", bufs=4))
+
+        ident = keep.tile([P, P], F32, name="ident")
+        make_identity(nc, ident[:])
+
+        raws = []
+        for b in range(BATCH):
+            raw_b = keep.tile([P, 2, PACK, HALF], BF16, name="raw%d" % b)
+            raws.append(raw_b)
+        s_raws = []
+        s_grps = []
+        for s in range(NSUP):
+            s_raw = keep.tile([P, PACK * NODES], BF16, name="sraw%d" % s)
+            s_raws.append(s_raw)
+            s_grp = keep.tile([P, PACK * NODES], BF16, name="sgrp%d" % s, align_bytes=64)
+            s_grps.append(s_grp)
+        s_codes = keep.tile([P, NSUP, NODES], U32, name="scodes", align_bytes=64)
+        s_scales = keep.tile([P, NSUP, NODES], U8, name="sscales", align_bytes=64)
+        x0_codes = keep.tile([P, BATCH, FEAT], U32, name="x0codes", align_bytes=64)
+        x0_scales = keep.tile([P, BATCH, FEAT], U8, name="x0scales", align_bytes=64)
+
+        out_views = [out[b].rearrange("(p m) c -> p m c", m=PACK) for b in range(BATCH)]
+
+        def load_x0(b):
+            nc.sync.dma_start(out=raws[b][:, 0], in_=x[b].rearrange("(p m) f -> p m f", m=PACK))
+            nc.sync.dma_start(out=raws[b][:, 1], in_=h[b].rearrange("(p m) f -> p m f", m=PACK))
+
+        def load_s(s):
+            nc.sync.dma_start(out=s_raws[s][:], in_=supports[s].rearrange("(c m) j -> c (m j)", m=PACK))
+
+        t_banks = {}
+
+        def transpose_s(s):
+            words = s_raws[s][:].bitcast(F32).rearrange("c (m w u) -> c m u w", m=PACK, u=2)
+            for k in range(2):
+                tp = ps_b.tile([P, 2, 2, P], F32, tag="b", name="tp%d%d" % (s, k))
+                for mm in range(2):
+                    for u in range(2):
+                        nc.tensor.transpose(tp[:, mm, u, :], words[:, 2 * k + mm, u, :], ident[:])
+                t_banks[(s, k)] = tp
+
+        def s_out(s, k, engine_copy):
+            dst = s_grps[s][:].bitcast(F32).rearrange("p (m c u) -> p m c u", m=PACK, u=2)
+            engine_copy(out=dst[:, 2 * k : 2 * k + 2], in_=t_banks[(s, k)][:].rearrange("p m u c -> p m c u"))
+
+        def quant_s(s):
+            nc.vector.quantize_mx(out=s_codes[:, s, :].bitcast(FP8X4), scales=s_scales[:, s, :], in_=s_grps[s][:])
+
+        g0s = {}
+
+        def regroup_x0(b):
+            g0 = g0_pool.tile([P, PACK * FEAT], BF16, tag="g0", name="g0_%d" % b, align_bytes=64)
+            nc.vector.tensor_copy(
+                out=g0[:].rearrange("p (s c i t) -> p s c t i", s=2, i=4, t=PACK),
+                in_=raws[b][:].rearrange("p s t (c i) -> p s c t i", i=4),
+            )
+            g0s[b] = g0
+
+        def quant_x0(b):
+            nc.vector.quantize_mx(out=x0_codes[:, b, :].bitcast(FP8X4), scales=x0_scales[:, b, :], in_=g0s[b][:])
+
+        def cast_x0(b, engine_copy):
+            st0 = st0_pool.tile([P, PACK, FEAT], F32, tag="st0", name="st0_%d" % b)
+            engine_copy(
+                out=st0[:].rearrange("p m (s f) -> p m s f", s=2),
+                in_=raws[b][:].rearrange("p s m f -> p m s f"),
+            )
+            nc.sync.dma_start(out=out_views[b][:, :, 0:FEAT], in_=st0[:])
+
+        a_banks = {}
+        stages = {}
+        g1s = {}
+        x1q = {}
+
+        def step1(u):
+            b, s = divmod(u, NSUP)
+            for g in range(PACK):
+                bank = ps_a.tile([P, PACK, CHUNK], F32, tag="a", name="a%d_%d" % (u, g))
+                cols = slice(g * CHUNK, (g + 1) * CHUNK)
+                for m in range(PACK):
+                    rows = slice(m * P, (m + 1) * P)
+                    nc.tensor.matmul_mx(
+                        out=bank[:, m, :],
+                        lhsT=s_codes[:, s, rows].bitcast(FP8X4),
+                        lhsT_scale=s_scales[:, s, rows],
+                        rhs=x0_codes[:, b, cols].bitcast(FP8X4),
+                        rhs_scale=x0_scales[:, b, cols],
+                        start=True,
+                        stop=True,
+                    )
+                a_banks[(u, g)] = bank
+
+        def drain1(u):
+            g1 = g1_pool.tile([P, PACK * FEAT], BF16, tag="g1", name="g1_%d" % u, align_bytes=64)
+            st = st_pool.tile([P, PACK, 2, FEAT], F32, tag="st", name="st_%d" % u)
+            for g in range(PACK):
+                nc.scalar.copy(
+                    out=g1[:, g * PACK * CHUNK : (g + 1) * PACK * CHUNK].rearrange("p (f m) -> p f m", m=PACK),
+                    in_=a_banks[(u, g)][:].rearrange("p m f -> p f m"),
+                )
+            for g in range(PACK):
+                nc.scalar.copy(out=st[:, :, 0, g * CHUNK : (g + 1) * CHUNK], in_=a_banks[(u, g)][:])
+            g1s[u] = g1
+            stages[u] = st
+
+        def quant_x1(u):
+            codes = g1_pool.tile([P, FEAT], U32, tag="x1c", name="x1c_%d" % u, align_bytes=64)
+            scales = g1_pool.tile([P, FEAT], U8, tag="x1s", name="x1s_%d" % u, align_bytes=64)
+            nc.vector.quantize_mx(out=codes[:].bitcast(FP8X4), scales=scales[:], in_=g1s[u][:])
+            x1q[u] = (codes, scales)
+
+        def step2(u):
+            b, s = divmod(u, NSUP)
+            codes, scales = x1q[u]
+            st = stages[u]
+            banks = []
+            for m in range(PACK):
+                rows = slice(m * P, (m + 1) * P)
+                bank = ps_b.tile([P, 2, HALF], F32, tag="b", name="b%d_%d" % (u, m))
+                nc.tensor.matmul_mx(
+                    out=bank[:].rearrange("p s f -> p (s f)"),
+                    lhsT=s_codes[:, s, rows].bitcast(FP8X4),
+                    lhsT_scale=s_scales[:, s, rows],
+                    rhs=codes[:].bitcast(FP8X4),
+                    rhs_scale=scales[:],
+                    start=True,
+                    stop=True,
+                )
+                banks.append(bank)
+            for m in range(PACK):
+                nc.vector.scalar_tensor_tensor(
+                    out=st[:, m, 1, :].rearrange("p (s f) -> p s f", s=2),
+                    in0=banks[m][:],
+                    scalar=2.0,
+                    in1=raws[b][:, :, m, :],
+                    op0=MULT,
+                    op1=SUBTRACT,
+                )
+            c0 = FEAT + s * 2 * FEAT
+            nc.sync.dma_start(out=out_views[b][:, :, c0 : c0 + 2 * FEAT], in_=st[:].rearrange("p m k f -> p m (k f)"))
+
+        load_x0(0)
+        load_s(0)
+        load_s(1)
+        for b in range(1, BATCH):
+            load_x0(b)
+
+        transpose_s(0)
+        transpose_s(1)
+
+        regroup_x0(0)
+        cast_x0(0, nc.scalar.copy)
+        quant_x0(0)
+        s_out(0, 0, nc.vector.tensor_copy)
+        s_out(0, 1, nc.scalar.copy)
+        quant_s(0)
+        step1(0)
+        s_out(1, 0, nc.vector.tensor_copy)
+        s_out(1, 1, nc.scalar.copy)
+        cast_x0(1, nc.vector.tensor_copy)
+        quant_s(1)
+        cast_x0(2, nc.vector.tensor_copy)
+
+        for u in range(UNITS):
+            drain1(u)
+            if u + 1 < UNITS:
+                step1(u + 1)
+            quant_x1(u)
+            if u == 0:
+                regroup_x0(1)
+                cast_x0(3, nc.vector.tensor_copy)
+                quant_x0(1)
+            if u == 1:
+                regroup_x0(2)
+            if u == 3:
+                regroup_x0(3)
+            step2(u)
+            if u == 1:
+                quant_x0(2)
+            if u == 3:
+                quant_x0(3)

@@ -24,7 +24,7 @@ OUT_COLS = 2560
 
 FLOPS = 2 * NSUP * 2 * BATCH * NODES * NODES * FEAT
 
-MANUAL = True
+MANUAL = False
 
 
 def tile_dcgrucell_pa_kernel(tc, x, h, support0, support1, out):

@@ -10,6 +10,7 @@ U8 = mybir.dt.uint8
 FP8X4 = mybir.dt.float8_e4m3fn_x4
 MULT = mybir.AluOpType.mult
 SUBTRACT = mybir.AluOpType.subtract
+ADD = mybir.AluOpType.add
 
 P = 128
 PACK = 4
@@ -24,7 +25,8 @@ OUT_COLS = 2560
 
 FLOPS = 2 * NSUP * 2 * BATCH * NODES * NODES * FEAT
 
-MANUAL = False
+MANUAL = True
+STORE_TILES = 2
 
 
 def tile_dcgrucell_pa_kernel(tc, x, h, support0, support1, out):
@@ -100,22 +102,40 @@ def tile_dcgrucell_pa_kernel(tc, x, h, support0, support1, out):
         def quant_x0(b):
             nc.vector.quantize_mx(out=x0_codes[:, b, :].bitcast(FP8X4), scales=x0_scales[:, b, :], in_=g0s[b][:])
 
-        def cast_x0(b, engine_copy):
-            st0 = st0_pool.tile([P, PACK, FEAT], F32, tag="st0", name="st0_%d" % b)
-            engine_copy(
-                out=st0[:].rearrange("p m (s f) -> p m s f", s=2),
-                in_=raws[b][:].rearrange("p s m f -> p m s f"),
-            )
-            nc.sync.dma_start(out=out_views[b][:, :, 0:FEAT], in_=st0[:])
+        st0s = {}
+
+        def cast_x0(b, half, engine):
+            if half == 0:
+                st0_new = st0_pool.tile([P, PACK, FEAT], F32, tag="st0", name="st0_%d" % b)
+                st0s[b] = st0_new
+            st0 = st0s[b]
+            tiles = slice(2 * half, 2 * half + 2)
+            if engine == "pool":
+                for m in (2 * half, 2 * half + 1):
+                    nc.gpsimd.tensor_scalar(
+                        out=st0[:, m, :].rearrange("p (s f) -> p s f", s=2),
+                        in0=raws[b][:, :, m, :],
+                        scalar1=1.0,
+                        scalar2=0.0,
+                        op0=MULT,
+                        op1=ADD,
+                    )
+            else:
+                copy = nc.scalar.copy if engine == "act" else nc.vector.tensor_copy
+                copy(
+                    out=st0[:, tiles, :].rearrange("p m (s f) -> p m s f", s=2),
+                    in_=raws[b][:, :, tiles, :].rearrange("p s m f -> p m s f"),
+                )
+            nc.sync.dma_start(out=out_views[b][:, tiles, 0:FEAT], in_=st0[:, tiles, :])
 
         a_banks = {}
         stages = {}
         g1s = {}
         x1q = {}
 
-        def step1(u):
+        def step1(u, chunks):
             b, s = divmod(u, NSUP)
-            for g in range(PACK):
+            for g in chunks:
                 bank = ps_a.tile([P, PACK, CHUNK], F32, tag="a", name="a%d_%d" % (u, g))
                 cols = slice(g * CHUNK, (g + 1) * CHUNK)
                 for m in range(PACK):
@@ -150,12 +170,12 @@ def tile_dcgrucell_pa_kernel(tc, x, h, support0, support1, out):
             nc.vector.quantize_mx(out=codes[:].bitcast(FP8X4), scales=scales[:], in_=g1s[u][:])
             x1q[u] = (codes, scales)
 
-        def step2(u):
+        b_banks = {}
+
+        def step2(u, tiles):
             b, s = divmod(u, NSUP)
             codes, scales = x1q[u]
-            st = stages[u]
-            banks = []
-            for m in range(PACK):
+            for m in tiles:
                 rows = slice(m * P, (m + 1) * P)
                 bank = ps_b.tile([P, 2, HALF], F32, tag="b", name="b%d_%d" % (u, m))
                 nc.tensor.matmul_mx(
@@ -167,18 +187,27 @@ def tile_dcgrucell_pa_kernel(tc, x, h, support0, support1, out):
                     start=True,
                     stop=True,
                 )
-                banks.append(bank)
+                b_banks[(u, m)] = bank
+
+        def drain2(u):
+            b, s = divmod(u, NSUP)
+            st = stages[u]
+            c0 = FEAT + s * 2 * FEAT
             for m in range(PACK):
                 nc.vector.scalar_tensor_tensor(
                     out=st[:, m, 1, :].rearrange("p (s f) -> p s f", s=2),
-                    in0=banks[m][:],
+                    in0=b_banks[(u, m)][:],
                     scalar=2.0,
                     in1=raws[b][:, :, m, :],
                     op0=MULT,
                     op1=SUBTRACT,
                 )
-            c0 = FEAT + s * 2 * FEAT
-            nc.sync.dma_start(out=out_views[b][:, :, c0 : c0 + 2 * FEAT], in_=st[:].rearrange("p m k f -> p m (k f)"))
+                if (m + 1) % STORE_TILES == 0:
+                    tiles = slice(m + 1 - STORE_TILES, m + 1)
+                    nc.sync.dma_start(
+                        out=out_views[b][:, tiles, c0 : c0 + 2 * FEAT],
+                        in_=st[:, tiles].rearrange("p m k f -> p m (k f)"),
+                    )
 
         load_x0(0)
         load_s(0)
@@ -190,32 +219,42 @@ def tile_dcgrucell_pa_kernel(tc, x, h, support0, support1, out):
         transpose_s(1)
 
         regroup_x0(0)
-        cast_x0(0, nc.scalar.copy)
+        cast_x0(0, 0, "act")
+        cast_x0(0, 1, "act")
         quant_x0(0)
         s_out(0, 0, nc.vector.tensor_copy)
         s_out(0, 1, nc.scalar.copy)
         quant_s(0)
-        step1(0)
+        step1(0, range(PACK))
+        cast_x0(1, 0, "dve")
+        cast_x0(1, 1, "dve")
         s_out(1, 0, nc.vector.tensor_copy)
         s_out(1, 1, nc.scalar.copy)
-        cast_x0(1, nc.vector.tensor_copy)
+        for b in (2, 3):
+            cast_x0(b, 0, "pool")
+            cast_x0(b, 1, "pool")
         quant_s(1)
-        cast_x0(2, nc.vector.tensor_copy)
+        regroup_x0(1)
 
         for u in range(UNITS):
             drain1(u)
             if u + 1 < UNITS:
-                step1(u + 1)
+                step1(u + 1, (0, 1))
             quant_x1(u)
             if u == 0:
-                regroup_x0(1)
-                cast_x0(3, nc.vector.tensor_copy)
                 quant_x0(1)
+            step2(u, (0,))
+            if u + 1 < UNITS:
+                step1(u + 1, (2,))
+            step2(u, (1,))
+            if u + 1 < UNITS:
+                step1(u + 1, (3,))
+            step2(u, (2, 3))
             if u == 1:
                 regroup_x0(2)
             if u == 3:
                 regroup_x0(3)
-            step2(u)
+            drain2(u)
             if u == 1:
                 quant_x0(2)
             if u == 3:

@@ -230,30 +230,25 @@ def tile_dcgrucell_pa_kernel(tc, x, h, support0, support1, out):
         cast_x0(1, 1, "dve")
         s_out(1, 0, nc.vector.tensor_copy)
         s_out(1, 1, nc.scalar.copy)
-        for b in (2, 3):
-            cast_x0(b, 0, "pool")
-            cast_x0(b, 1, "pool")
         quant_s(1)
-        regroup_x0(1)
+        cast_x0(2, 0, "dve")
+        cast_x0(2, 1, "dve")
 
         for u in range(UNITS):
             drain1(u)
             if u + 1 < UNITS:
-                step1(u + 1, (0, 1))
+                step1(u + 1, range(PACK))
             quant_x1(u)
             if u == 0:
+                regroup_x0(1)
+                cast_x0(3, 0, "dve")
+                cast_x0(3, 1, "dve")
                 quant_x0(1)
-            step2(u, (0,))
-            if u + 1 < UNITS:
-                step1(u + 1, (2,))
-            step2(u, (1,))
-            if u + 1 < UNITS:
-                step1(u + 1, (3,))
-            step2(u, (2, 3))
             if u == 1:
                 regroup_x0(2)
             if u == 3:
                 regroup_x0(3)
+            step2(u, range(PACK))
             drain2(u)
             if u == 1:
                 quant_x0(2)

@@ -26,7 +26,24 @@ OUT_COLS = 2560
 FLOPS = 2 * NSUP * 2 * BATCH * NODES * NODES * FEAT
 
 MANUAL = True
-STORE_TILES = 2
+
+X1 = FEAT
+BOTH = 2 * FEAT
+UNIT_TILES = (4, 2, 1, 0)
+
+
+def store_plan(b):
+    j = UNIT_TILES[b]
+    plan = []
+    for s in range(NSUP):
+        c = FEAT + s * BOTH
+        if j == 4:
+            plan.extend([(s, 1, 0, 2, c, BOTH), (s, 3, 2, 2, c, BOTH)])
+        elif j > 0:
+            plan.append((s, j - 1, 0, j, c, BOTH))
+    for t in range(j, PACK):
+        plan.append((1, t, t, 1, FEAT, 2 * BOTH))
+    return plan
 
 
 def tile_dcgrucell_pa_kernel(tc, x, h, support0, support1, out):
@@ -37,9 +54,7 @@ def tile_dcgrucell_pa_kernel(tc, x, h, support0, support1, out):
             ctx.enter_context(tc.manual_schedule())
         keep = ctx.enter_context(tc.tile_pool(name="keep", bufs=1))
         g0_pool = ctx.enter_context(tc.tile_pool(name="g0p", bufs=2))
-        g1_pool = ctx.enter_context(tc.tile_pool(name="g1p", bufs=3))
-        st0_pool = ctx.enter_context(tc.tile_pool(name="st0p", bufs=4))
-        st_pool = ctx.enter_context(tc.tile_pool(name="stp", bufs=6))
+        g1_pool = ctx.enter_context(tc.tile_pool(name="g1p", bufs=2))
         ps_a = ctx.enter_context(tc.psum_pool(name="psa", bufs=4))
         ps_b = ctx.enter_context(tc.psum_pool(name="psb", bufs=4))
 
@@ -47,9 +62,12 @@ def tile_dcgrucell_pa_kernel(tc, x, h, support0, support1, out):
         make_identity(nc, ident[:])
 
         raws = []
+        rows = []
         for b in range(BATCH):
             raw_b = keep.tile([P, 2, PACK, HALF], BF16, name="raw%d" % b)
             raws.append(raw_b)
+            rows_b = keep.tile([P, PACK, OUT_COLS], F32, name="rows%d" % b)
+            rows.append(rows_b)
         s_raws = []
         s_grps = []
         for s in range(NSUP):
@@ -102,18 +120,13 @@ def tile_dcgrucell_pa_kernel(tc, x, h, support0, support1, out):
         def quant_x0(b):
             nc.vector.quantize_mx(out=x0_codes[:, b, :].bitcast(FP8X4), scales=x0_scales[:, b, :], in_=g0s[b][:])
 
-        st0s = {}
-
         def cast_x0(b, half, engine):
-            if half == 0:
-                st0_new = st0_pool.tile([P, PACK, FEAT], F32, tag="st0", name="st0_%d" % b)
-                st0s[b] = st0_new
-            st0 = st0s[b]
+            st0 = rows[b]
             tiles = slice(2 * half, 2 * half + 2)
             if engine == "pool":
                 for m in (2 * half, 2 * half + 1):
                     nc.gpsimd.tensor_scalar(
-                        out=st0[:, m, :].rearrange("p (s f) -> p s f", s=2),
+                        out=st0[:, m, 0:FEAT].rearrange("p (s f) -> p s f", s=2),
                         in0=raws[b][:, :, m, :],
                         scalar1=1.0,
                         scalar2=0.0,
@@ -123,13 +136,12 @@ def tile_dcgrucell_pa_kernel(tc, x, h, support0, support1, out):
             else:
                 copy = nc.scalar.copy if engine == "act" else nc.vector.tensor_copy
                 copy(
-                    out=st0[:, tiles, :].rearrange("p m (s f) -> p m s f", s=2),
+                    out=st0[:, tiles, 0:FEAT].rearrange("p m (s f) -> p m s f", s=2),
                     in_=raws[b][:, :, tiles, :].rearrange("p s m f -> p m s f"),
                 )
-            nc.sync.dma_start(out=out_views[b][:, tiles, 0:FEAT], in_=st0[:, tiles, :])
+            nc.sync.dma_start(out=out_views[b][:, tiles, 0:FEAT], in_=st0[:, tiles, 0:FEAT])
 
         a_banks = {}
-        stages = {}
         g1s = {}
         x1q = {}
 
@@ -152,17 +164,17 @@ def tile_dcgrucell_pa_kernel(tc, x, h, support0, support1, out):
                 a_banks[(u, g)] = bank
 
         def drain1(u):
+            b, s = divmod(u, NSUP)
+            c0 = FEAT + s * BOTH
             g1 = g1_pool.tile([P, PACK * FEAT], BF16, tag="g1", name="g1_%d" % u, align_bytes=64)
-            st = st_pool.tile([P, PACK, 2, FEAT], F32, tag="st", name="st_%d" % u)
             for g in range(PACK):
                 nc.scalar.copy(
                     out=g1[:, g * PACK * CHUNK : (g + 1) * PACK * CHUNK].rearrange("p (f m) -> p f m", m=PACK),
                     in_=a_banks[(u, g)][:].rearrange("p m f -> p f m"),
                 )
             for g in range(PACK):
-                nc.scalar.copy(out=st[:, :, 0, g * CHUNK : (g + 1) * CHUNK], in_=a_banks[(u, g)][:])
+                nc.scalar.copy(out=rows[b][:, :, c0 + g * CHUNK : c0 + (g + 1) * CHUNK], in_=a_banks[(u, g)][:])
             g1s[u] = g1
-            stages[u] = st
 
         def quant_x1(u):
             codes = g1_pool.tile([P, FEAT], U32, tag="x1c", name="x1c_%d" % u, align_bytes=64)
@@ -191,23 +203,22 @@ def tile_dcgrucell_pa_kernel(tc, x, h, support0, support1, out):
 
         def drain2(u):
             b, s = divmod(u, NSUP)
-            st = stages[u]
-            c0 = FEAT + s * 2 * FEAT
+            c0 = FEAT + s * BOTH + X1
             for m in range(PACK):
                 nc.vector.scalar_tensor_tensor(
-                    out=st[:, m, 1, :].rearrange("p (s f) -> p s f", s=2),
+                    out=rows[b][:, m, c0 : c0 + FEAT].rearrange("p (s f) -> p s f", s=2),
                     in0=b_banks[(u, m)][:],
                     scalar=2.0,
                     in1=raws[b][:, :, m, :],
                     op0=MULT,
                     op1=SUBTRACT,
                 )
-                if (m + 1) % STORE_TILES == 0:
-                    tiles = slice(m + 1 - STORE_TILES, m + 1)
-                    nc.sync.dma_start(
-                        out=out_views[b][:, tiles, c0 : c0 + 2 * FEAT],
-                        in_=st[:, tiles].rearrange("p m k f -> p m (k f)"),
-                    )
+                for after_s, after_m, t0, nt, col, ncol in store_plan(b):
+                    if after_s == s and after_m == m:
+                        nc.sync.dma_start(
+                            out=out_views[b][:, t0 : t0 + nt, col : col + ncol],
+                            in_=rows[b][:, t0 : t0 + nt, col : col + ncol],
+                        )
 
         load_x0(0)
         load_s(0)

@@ -29,7 +29,7 @@ MANUAL = True
 
 X1 = FEAT
 BOTH = 2 * FEAT
-UNIT_TILES = (4, 2, 1, 0)
+UNIT_TILES = (4, 4, 2, 1)
 
 
 def store_plan(b):

@@ -41,8 +41,10 @@ def store_plan(b):
             plan.extend([(s, 1, 0, 2, c, BOTH), (s, 3, 2, 2, c, BOTH)])
         elif j > 0:
             plan.append((s, j - 1, 0, j, c, BOTH))
-    for t in range(j, PACK):
-        plan.append((1, t, t, 1, FEAT, 2 * BOTH))
+    if j % 2 == 1:
+        plan.append((1, j, j, 1, FEAT, 2 * BOTH))
+    for t in range(j + j % 2, PACK, 2):
+        plan.append((1, t + 1, t, 2, FEAT, 2 * BOTH))
     return plan
 
 

@@ -27,6 +27,8 @@ FLOPS = 2 * NSUP * 2 * BATCH * NODES * NODES * FEAT
 
 MANUAL = True
 
+POOL_CHUNKS = 2
+
 X1 = FEAT
 BOTH = 2 * FEAT
 UNIT_TILES = (4, 4, 2, 1)
@@ -169,13 +171,27 @@ def tile_dcgrucell_pa_kernel(tc, x, h, support0, support1, out):
             b, s = divmod(u, NSUP)
             c0 = FEAT + s * BOTH
             g1 = g1_pool.tile([P, PACK * FEAT], BF16, tag="g1", name="g1_%d" % u, align_bytes=64)
-            for g in range(PACK):
-                nc.scalar.copy(
-                    out=g1[:, g * PACK * CHUNK : (g + 1) * PACK * CHUNK].rearrange("p (f m) -> p f m", m=PACK),
-                    in_=a_banks[(u, g)][:].rearrange("p m f -> p f m"),
+
+            def regrouped(g):
+                return g1[:, g * PACK * CHUNK : (g + 1) * PACK * CHUNK].rearrange("p (f m) -> p f m", m=PACK)
+
+            def staged(g):
+                return rows[b][:, :, c0 + g * CHUNK : c0 + (g + 1) * CHUNK]
+
+            for g in range(POOL_CHUNKS):
+                nc.scalar.copy(out=staged(g), in_=a_banks[(u, g)][:])
+                nc.gpsimd.tensor_scalar(
+                    out=regrouped(g),
+                    in0=staged(g).rearrange("p m f -> p f m"),
+                    scalar1=1.0,
+                    scalar2=0.0,
+                    op0=MULT,
+                    op1=ADD,
                 )
-            for g in range(PACK):
-                nc.scalar.copy(out=rows[b][:, :, c0 + g * CHUNK : c0 + (g + 1) * CHUNK], in_=a_banks[(u, g)][:])
+            for g in range(POOL_CHUNKS, PACK):
+                nc.scalar.copy(out=regrouped(g), in_=a_banks[(u, g)][:].rearrange("p m f -> p f m"))
+            for g in range(POOL_CHUNKS, PACK):
+                nc.scalar.copy(out=staged(g), in_=a_banks[(u, g)][:])
             g1s[u] = g1
 
         def quant_x1(u):

@@ -31,23 +31,24 @@ POOL_CHUNKS = 2
 
 X1 = FEAT
 BOTH = 2 * FEAT
-UNIT_TILES = (4, 4, 2, 1)
+UNIT0 = FEAT
+UNIT1 = FEAT + BOTH
 
-
-def store_plan(b):
-    j = UNIT_TILES[b]
-    plan = []
-    for s in range(NSUP):
-        c = FEAT + s * BOTH
-        if j == 4:
-            plan.extend([(s, 1, 0, 2, c, BOTH), (s, 3, 2, 2, c, BOTH)])
-        elif j > 0:
-            plan.append((s, j - 1, 0, j, c, BOTH))
-    if j % 2 == 1:
-        plan.append((1, j, j, 1, FEAT, 2 * BOTH))
-    for t in range(j + j % 2, PACK, 2):
-        plan.append((1, t + 1, t, 2, FEAT, 2 * BOTH))
-    return plan
+STORES = {
+    (0, 1): [(0, 2, UNIT0, BOTH)],
+    (0, 3): [(2, 2, UNIT0, BOTH)],
+    (1, 1): [(0, 2, UNIT1, BOTH)],
+    (1, 3): [(2, 2, UNIT1, BOTH)],
+    (2, 1): [(0, 2, UNIT0, BOTH)],
+    (2, 3): [(2, 2, UNIT0, BOTH)],
+    (3, 1): [(0, 2, UNIT1, BOTH)],
+    (3, 3): [(2, 2, UNIT1, BOTH)],
+    (4, 1): [(0, 2, UNIT0, BOTH)],
+    (5, 1): [(0, 2, UNIT1, BOTH)],
+    (5, 3): [(2, 2, 0, OUT_COLS)],
+    (7, 1): [(0, 2, 0, OUT_COLS)],
+    (7, 3): [(2, 2, 0, OUT_COLS)],
+}
 
 
 def tile_dcgrucell_pa_kernel(tc, x, h, support0, support1, out):
@@ -113,18 +114,39 @@ def tile_dcgrucell_pa_kernel(tc, x, h, support0, support1, out):
 
         g0s = {}
 
-        def regroup_x0(b):
-            g0 = g0_pool.tile([P, PACK * FEAT], BF16, tag="g0", name="g0_%d" % b, align_bytes=64)
-            nc.vector.tensor_copy(
-                out=g0[:].rearrange("p (s c i t) -> p s c t i", s=2, i=4, t=PACK),
-                in_=raws[b][:].rearrange("p s t (c i) -> p s c t i", i=4),
+        def regroup_x0(b, engine, parts):
+            if b not in g0s:
+                g0_b = g0_pool.tile([P, 2, PACK * HALF], BF16, tag="g0", name="g0_%d" % b, align_bytes=64)
+                g0s[b] = g0_b
+            g0 = g0s[b]
+            for part in parts:
+                if engine == "dve":
+                    nc.vector.tensor_copy(
+                        out=g0[:, part, :].rearrange("p (c i t) -> p c t i", i=4, t=PACK),
+                        in_=raws[b][:, part].rearrange("p t (c i) -> p c t i", i=4),
+                    )
+                else:
+                    for k in range(2):
+                        f = slice(k * CHUNK, (k + 1) * CHUNK)
+                        nc.gpsimd.tensor_scalar(
+                            out=g0[:, part, k * PACK * CHUNK : (k + 1) * PACK * CHUNK].rearrange("p (f t) -> p f t", t=PACK),
+                            in0=raws[b][:, part, :, f].rearrange("p t f -> p f t"),
+                            scalar1=1.0,
+                            scalar2=0.0,
+                            op0=MULT,
+                            op1=ADD,
+                        )
+
+        def quant_x0(b, parts=(0, 2)):
+            p0, p1 = parts
+            cols = slice(p0 * HALF, p1 * HALF)
+            nc.vector.quantize_mx(
+                out=x0_codes[:, b, cols].bitcast(FP8X4),
+                scales=x0_scales[:, b, cols],
+                in_=g0s[b][:, p0:p1, :].rearrange("p s w -> p (s w)"),
             )
-            g0s[b] = g0
 
-        def quant_x0(b):
-            nc.vector.quantize_mx(out=x0_codes[:, b, :].bitcast(FP8X4), scales=x0_scales[:, b, :], in_=g0s[b][:])
-
-        def cast_x0(b, half, engine):
+        def cast_x0(b, half, engine, store=False):
             st0 = rows[b]
             tiles = slice(2 * half, 2 * half + 2)
             if engine == "pool":
@@ -143,7 +165,8 @@ def tile_dcgrucell_pa_kernel(tc, x, h, support0, support1, out):
                     out=st0[:, tiles, 0:FEAT].rearrange("p m (s f) -> p m s f", s=2),
                     in_=raws[b][:, :, tiles, :].rearrange("p s m f -> p m s f"),
                 )
-            nc.sync.dma_start(out=out_views[b][:, tiles, 0:FEAT], in_=st0[:, tiles, 0:FEAT])
+            if store:
+                nc.sync.dma_start(out=out_views[b][:, tiles, 0:FEAT], in_=st0[:, tiles, 0:FEAT])
 
         a_banks = {}
         g1s = {}
@@ -178,7 +201,8 @@ def tile_dcgrucell_pa_kernel(tc, x, h, support0, support1, out):
             def staged(g):
                 return rows[b][:, :, c0 + g * CHUNK : c0 + (g + 1) * CHUNK]
 
-            for g in range(POOL_CHUNKS):
+            pool_chunks = POOL_CHUNKS if u > 0 else 0
+            for g in range(pool_chunks):
                 nc.scalar.copy(out=staged(g), in_=a_banks[(u, g)][:])
                 nc.gpsimd.tensor_scalar(
                     out=regrouped(g),
@@ -188,9 +212,9 @@ def tile_dcgrucell_pa_kernel(tc, x, h, support0, support1, out):
                     op0=MULT,
                     op1=ADD,
                 )
-            for g in range(POOL_CHUNKS, PACK):
+            for g in range(pool_chunks, PACK):
                 nc.scalar.copy(out=regrouped(g), in_=a_banks[(u, g)][:].rearrange("p m f -> p f m"))
-            for g in range(POOL_CHUNKS, PACK):
+            for g in range(pool_chunks, PACK):
                 nc.scalar.copy(out=staged(g), in_=a_banks[(u, g)][:])
             g1s[u] = g1
 
@@ -231,55 +255,64 @@ def tile_dcgrucell_pa_kernel(tc, x, h, support0, support1, out):
                     op0=MULT,
                     op1=SUBTRACT,
                 )
-                for after_s, after_m, t0, nt, col, ncol in store_plan(b):
-                    if after_s == s and after_m == m:
-                        nc.sync.dma_start(
-                            out=out_views[b][:, t0 : t0 + nt, col : col + ncol],
-                            in_=rows[b][:, t0 : t0 + nt, col : col + ncol],
-                        )
+                for t0, nt, col, ncol in STORES.get((u, m), []):
+                    nc.sync.dma_start(
+                        out=out_views[b][:, t0 : t0 + nt, col : col + ncol],
+                        in_=rows[b][:, t0 : t0 + nt, col : col + ncol],
+                    )
 
-        load_x0(0)
+        warm = keep.tile([P, 2], F32, name="warm")
+        nc.vector.memset(warm[:], 0.0)
+        nc.scalar.copy(out=warm[:, 1:2], in_=warm[:, 0:1])
+
         load_s(0)
+        load_x0(0)
         load_s(1)
         for b in range(1, BATCH):
             load_x0(b)
 
         transpose_s(0)
         transpose_s(1)
-
-        regroup_x0(0)
-        cast_x0(0, 0, "act")
-        cast_x0(0, 1, "act")
-        quant_x0(0)
-        s_out(0, 0, nc.vector.tensor_copy)
+        s_out(0, 0, nc.scalar.copy)
         s_out(0, 1, nc.scalar.copy)
+        regroup_x0(0, "dve", range(2))
+        quant_x0(0, (0, 1))
         quant_s(0)
+        quant_x0(0, (1, 2))
+        cast_x0(0, 0, "act", store=True)
         step1(0, range(PACK))
-        cast_x0(1, 0, "dve")
-        cast_x0(1, 1, "dve")
         s_out(1, 0, nc.vector.tensor_copy)
-        s_out(1, 1, nc.scalar.copy)
+        s_out(1, 1, nc.vector.tensor_copy)
+        cast_x0(0, 1, "dve", store=True)
         quant_s(1)
-        cast_x0(2, 0, "dve")
-        cast_x0(2, 1, "dve")
+        cast_x0(1, 0, "dve", store=True)
+        cast_x0(1, 1, "dve", store=True)
+        regroup_x0(1, "pool", range(2))
+        regroup_x0(2, "pool", range(2))
+
+        def vector_filler(u):
+            if u == 0:
+                quant_x0(1)
+            elif u == 2:
+                quant_x0(2)
+            elif u == 3:
+                cast_x0(2, 1, "dve")
+            elif u == 4:
+                quant_x0(3)
+            elif u == 5 or u == 6:
+                cast_x0(3, u - 5, "dve")
 
         for u in range(UNITS):
             drain1(u)
-            if u + 1 < UNITS:
+            if u == 1 or u == 2:
+                regroup_x0(3, "pool", [u - 1])
+            if u > 0 and u + 1 < UNITS:
                 step1(u + 1, range(PACK))
             quant_x1(u)
-            if u == 0:
-                regroup_x0(1)
-                cast_x0(3, 0, "dve")
-                cast_x0(3, 1, "dve")
-                quant_x0(1)
-            if u == 1:
-                regroup_x0(2)
-            if u == 3:
-                regroup_x0(3)
             step2(u, range(PACK))
+            if u == 0:
+                step1(1, range(PACK))
+            vector_filler(u)
             drain2(u)
-            if u == 1:
-                quant_x0(2)
-            if u == 3:
-                quant_x0(3)
+            if u == 0:
+                cast_x0(2, 0, "dve", store=True)

@@ -10,7 +10,6 @@ U8 = mybir.dt.uint8
 FP8X4 = mybir.dt.float8_e4m3fn_x4
 MULT = mybir.AluOpType.mult
 SUBTRACT = mybir.AluOpType.subtract
-ADD = mybir.AluOpType.add
 
 P = 128
 PACK = 4
@@ -27,8 +26,6 @@ FLOPS = 2 * NSUP * 2 * BATCH * NODES * NODES * FEAT
 
 MANUAL = True
 
-POOL_CHUNKS = 2
-
 X1 = FEAT
 BOTH = 2 * FEAT
 UNIT0 = FEAT
@@ -40,14 +37,13 @@ STORES = {
     (1, 1): [(0, 2, UNIT1, BOTH)],
     (1, 3): [(2, 2, UNIT1, BOTH)],
     (2, 1): [(0, 2, UNIT0, BOTH)],
-    (2, 3): [(2, 2, UNIT0, BOTH)],
     (3, 1): [(0, 2, UNIT1, BOTH)],
-    (3, 3): [(2, 2, UNIT1, BOTH)],
+    (3, 3): [(2, 2, UNIT0, 2 * BOTH)],
     (4, 1): [(0, 2, UNIT0, BOTH)],
     (5, 1): [(0, 2, UNIT1, BOTH)],
-    (5, 3): [(2, 2, 0, OUT_COLS)],
-    (7, 1): [(0, 2, 0, OUT_COLS)],
-    (7, 3): [(2, 2, 0, OUT_COLS)],
+    (5, 3): [(2, 2, UNIT0, 2 * BOTH)],
+    (7, 1): [(0, 2, UNIT0, 2 * BOTH)],
+    (7, 3): [(2, 2, UNIT0, 2 * BOTH)],
 }
 
 
@@ -114,28 +110,16 @@ def tile_dcgrucell_pa_kernel(tc, x, h, support0, support1, out):
 
         g0s = {}
 
-        def regroup_x0(b, engine, parts):
+        def regroup_x0(b, parts=(0, 1)):
             if b not in g0s:
                 g0_b = g0_pool.tile([P, 2, PACK * HALF], BF16, tag="g0", name="g0_%d" % b, align_bytes=64)
                 g0s[b] = g0_b
             g0 = g0s[b]
             for part in parts:
-                if engine == "dve":
-                    nc.vector.tensor_copy(
-                        out=g0[:, part, :].rearrange("p (c i t) -> p c t i", i=4, t=PACK),
-                        in_=raws[b][:, part].rearrange("p t (c i) -> p c t i", i=4),
-                    )
-                else:
-                    for k in range(2):
-                        f = slice(k * CHUNK, (k + 1) * CHUNK)
-                        nc.gpsimd.tensor_scalar(
-                            out=g0[:, part, k * PACK * CHUNK : (k + 1) * PACK * CHUNK].rearrange("p (f t) -> p f t", t=PACK),
-                            in0=raws[b][:, part, :, f].rearrange("p t f -> p f t"),
-                            scalar1=1.0,
-                            scalar2=0.0,
-                            op0=MULT,
-                            op1=ADD,
-                        )
+                nc.vector.tensor_copy(
+                    out=g0[:, part, :].rearrange("p (c i t) -> p c t i", i=4, t=PACK),
+                    in_=raws[b][:, part].rearrange("p t (c i) -> p c t i", i=4),
+                )
 
         def quant_x0(b, parts=(0, 2)):
             p0, p1 = parts
@@ -149,22 +133,11 @@ def tile_dcgrucell_pa_kernel(tc, x, h, support0, support1, out):
         def cast_x0(b, half, engine, store=False):
             st0 = rows[b]
             tiles = slice(2 * half, 2 * half + 2)
-            if engine == "pool":
-                for m in (2 * half, 2 * half + 1):
-                    nc.gpsimd.tensor_scalar(
-                        out=st0[:, m, 0:FEAT].rearrange("p (s f) -> p s f", s=2),
-                        in0=raws[b][:, :, m, :],
-                        scalar1=1.0,
-                        scalar2=0.0,
-                        op0=MULT,
-                        op1=ADD,
-                    )
-            else:
-                copy = nc.scalar.copy if engine == "act" else nc.vector.tensor_copy
-                copy(
-                    out=st0[:, tiles, 0:FEAT].rearrange("p m (s f) -> p m s f", s=2),
-                    in_=raws[b][:, :, tiles, :].rearrange("p s m f -> p m s f"),
-                )
+            copy = nc.scalar.copy if engine == "act" else nc.vector.tensor_copy
+            copy(
+                out=st0[:, tiles, 0:FEAT].rearrange("p m (s f) -> p m s f", s=2),
+                in_=raws[b][:, :, tiles, :].rearrange("p s m f -> p m s f"),
+            )
             if store:
                 nc.sync.dma_start(out=out_views[b][:, tiles, 0:FEAT], in_=st0[:, tiles, 0:FEAT])
 
@@ -195,27 +168,13 @@ def tile_dcgrucell_pa_kernel(tc, x, h, support0, support1, out):
             c0 = FEAT + s * BOTH
             g1 = g1_pool.tile([P, PACK * FEAT], BF16, tag="g1", name="g1_%d" % u, align_bytes=64)
 
-            def regrouped(g):
-                return g1[:, g * PACK * CHUNK : (g + 1) * PACK * CHUNK].rearrange("p (f m) -> p f m", m=PACK)
-
-            def staged(g):
-                return rows[b][:, :, c0 + g * CHUNK : c0 + (g + 1) * CHUNK]
-
-            pool_chunks = POOL_CHUNKS if u > 0 else 0
-            for g in range(pool_chunks):
-                nc.scalar.copy(out=staged(g), in_=a_banks[(u, g)][:])
-                nc.gpsimd.tensor_scalar(
-                    out=regrouped(g),
-                    in0=staged(g).rearrange("p m f -> p f m"),
-                    scalar1=1.0,
-                    scalar2=0.0,
-                    op0=MULT,
-                    op1=ADD,
+            for g in range(PACK):
+                nc.scalar.copy(
+                    out=g1[:, g * PACK * CHUNK : (g + 1) * PACK * CHUNK].rearrange("p (f m) -> p f m", m=PACK),
+                    in_=a_banks[(u, g)][:].rearrange("p m f -> p f m"),
                 )
-            for g in range(pool_chunks, PACK):
-                nc.scalar.copy(out=regrouped(g), in_=a_banks[(u, g)][:].rearrange("p m f -> p f m"))
-            for g in range(pool_chunks, PACK):
-                nc.scalar.copy(out=staged(g), in_=a_banks[(u, g)][:])
+            for g in range(PACK):
+                nc.scalar.copy(out=rows[b][:, :, c0 + g * CHUNK : c0 + (g + 1) * CHUNK], in_=a_banks[(u, g)][:])
             g1s[u] = g1
 
         def quant_x1(u):
@@ -271,48 +230,52 @@ def tile_dcgrucell_pa_kernel(tc, x, h, support0, support1, out):
         for b in range(1, BATCH):
             load_x0(b)
 
+        zeros = keep.tile([P, FEAT], BF16, name="zeros")
+        nc.vector.memset(zeros[:], 0.0)
+
+        def keep_busy(pool, tag, count, n):
+            idle = pool.tile([P, FEAT], F32, tag=tag, name="idle%d" % n)
+            for i in range(count):
+                nc.tensor.matmul(idle[:], lhsT=zeros[:, 0:P], rhs=zeros[:], start=True, stop=True)
+
+        keep_busy(ps_a, "a", 8, 0)
         transpose_s(0)
-        transpose_s(1)
+        keep_busy(ps_a, "a", 2, 1)
         s_out(0, 0, nc.scalar.copy)
         s_out(0, 1, nc.scalar.copy)
-        regroup_x0(0, "dve", range(2))
+        regroup_x0(0)
         quant_x0(0, (0, 1))
         quant_s(0)
         quant_x0(0, (1, 2))
-        cast_x0(0, 0, "act", store=True)
         step1(0, range(PACK))
+        transpose_s(1)
+        cast_x0(0, 0, "dve", store=True)
+        cast_x0(0, 1, "dve", store=True)
+        cast_x0(1, 0, "dve", store=True)
         s_out(1, 0, nc.vector.tensor_copy)
         s_out(1, 1, nc.vector.tensor_copy)
-        cast_x0(0, 1, "dve", store=True)
         quant_s(1)
-        cast_x0(1, 0, "dve", store=True)
         cast_x0(1, 1, "dve", store=True)
-        regroup_x0(1, "pool", range(2))
-        regroup_x0(2, "pool", range(2))
-
-        def vector_filler(u):
-            if u == 0:
-                quant_x0(1)
-            elif u == 2:
-                quant_x0(2)
-            elif u == 3:
-                cast_x0(2, 1, "dve")
-            elif u == 4:
-                quant_x0(3)
-            elif u == 5 or u == 6:
-                cast_x0(3, u - 5, "dve")
 
         for u in range(UNITS):
             drain1(u)
-            if u == 1 or u == 2:
-                regroup_x0(3, "pool", [u - 1])
-            if u > 0 and u + 1 < UNITS:
+            if u + 1 < UNITS:
                 step1(u + 1, range(PACK))
             quant_x1(u)
             step2(u, range(PACK))
             if u == 0:
-                step1(1, range(PACK))
-            vector_filler(u)
-            drain2(u)
-            if u == 0:
                 cast_x0(2, 0, "dve", store=True)
+                cast_x0(2, 1, "dve", store=True)
+                regroup_x0(1)
+                quant_x0(1)
+                cast_x0(3, 0, "dve", store=True)
+                cast_x0(3, 1, "dve", store=True)
+            elif u == 1:
+                regroup_x0(2)
+            elif u == 2:
+                quant_x0(2)
+            elif u == 3:
+                regroup_x0(3)
+            elif u == 4:
+                quant_x0(3)
+            drain2(u)

@@ -92,9 +92,9 @@ def tile_dcgrucell_pa_kernel(tc, x, h, support0, support1, out):
 
         t_banks = {}
 
-        def transpose_s(s):
+        def transpose_s(s, halves=(0, 1)):
             words = s_raws[s][:].bitcast(F32).rearrange("c (m w u) -> c m u w", m=PACK, u=2)
-            for k in range(2):
+            for k in halves:
                 tp = ps_b.tile([P, 2, 2, P], F32, tag="b", name="tp%d%d" % (s, k))
                 for mm in range(2):
                     for u in range(2):
@@ -230,42 +230,43 @@ def tile_dcgrucell_pa_kernel(tc, x, h, support0, support1, out):
         for b in range(1, BATCH):
             load_x0(b)
 
-        zeros = keep.tile([P, FEAT], BF16, name="zeros")
-        nc.vector.memset(zeros[:], 0.0)
-
-        def keep_busy(pool, tag, count, n):
-            idle = pool.tile([P, FEAT], F32, tag=tag, name="idle%d" % n)
-            for i in range(count):
-                nc.tensor.matmul(idle[:], lhsT=zeros[:, 0:P], rhs=zeros[:], start=True, stop=True)
-
-        keep_busy(ps_a, "a", 8, 0)
         transpose_s(0)
-        keep_busy(ps_a, "a", 2, 1)
+        transpose_s(1, (0,))
         s_out(0, 0, nc.scalar.copy)
         s_out(0, 1, nc.scalar.copy)
         regroup_x0(0)
         quant_x0(0, (0, 1))
+        cast_x0(0, 0, "dve", store=True)
         quant_s(0)
         quant_x0(0, (1, 2))
+        cast_x0(0, 1, "act", store=True)
         step1(0, range(PACK))
-        transpose_s(1)
-        cast_x0(0, 0, "dve", store=True)
-        cast_x0(0, 1, "dve", store=True)
-        cast_x0(1, 0, "dve", store=True)
+        transpose_s(1, (1,))
         s_out(1, 0, nc.vector.tensor_copy)
-        s_out(1, 1, nc.vector.tensor_copy)
-        quant_s(1)
+        cast_x0(1, 0, "dve", store=True)
         cast_x0(1, 1, "dve", store=True)
+        cast_x0(2, 0, "dve", store=True)
+        cast_x0(2, 1, "dve", store=True)
 
         for u in range(UNITS):
             drain1(u)
-            if u + 1 < UNITS:
-                step1(u + 1, range(PACK))
-            quant_x1(u)
-            step2(u, range(PACK))
             if u == 0:
-                cast_x0(2, 0, "dve", store=True)
-                cast_x0(2, 1, "dve", store=True)
+                quant_x1(u)
+                s_out(1, 1, nc.vector.tensor_copy)
+                quant_s(1)
+            if u >= 1:
+                quant_x1(u)
+                for banks, tiles in (([0, 1], [0]), ([2], [1]), ([3], [2, 3])):
+                    if u + 1 < UNITS:
+                        step1(u + 1, banks)
+                    step2(u, tiles)
+            else:
+                if u + 1 < UNITS:
+                    step1(u + 1, range(PACK))
+                if u > 0:
+                    quant_x1(u)
+                step2(u, range(PACK))
+            if u == 0:
                 regroup_x0(1)
                 quant_x0(1)
                 cast_x0(3, 0, "dve", store=True)

@@ -10,6 +10,7 @@ U8 = mybir.dt.uint8
 FP8X4 = mybir.dt.float8_e4m3fn_x4
 MULT = mybir.AluOpType.mult
 SUBTRACT = mybir.AluOpType.subtract
+ADD = mybir.AluOpType.add
 
 P = 128
 PACK = 4
@@ -39,12 +40,16 @@ STORES = {
     (2, 1): [(0, 2, UNIT0, BOTH)],
     (3, 1): [(0, 2, UNIT1, BOTH)],
     (3, 3): [(2, 2, UNIT0, 2 * BOTH)],
-    (4, 1): [(0, 2, UNIT0, BOTH)],
-    (5, 1): [(0, 2, UNIT1, BOTH)],
+    (5, 1): [(0, 2, UNIT0, 2 * BOTH)],
     (5, 3): [(2, 2, UNIT0, 2 * BOTH)],
     (7, 1): [(0, 2, UNIT0, 2 * BOTH)],
     (7, 3): [(2, 2, UNIT0, 2 * BOTH)],
 }
+REGROUP = "pool"
+
+
+def vector_chunks(u):
+    return 1 if u >= 1 else 0
 
 
 def tile_dcgrucell_pa_kernel(tc, x, h, support0, support1, out):
@@ -54,7 +59,7 @@ def tile_dcgrucell_pa_kernel(tc, x, h, support0, support1, out):
         if MANUAL:
             ctx.enter_context(tc.manual_schedule())
         keep = ctx.enter_context(tc.tile_pool(name="keep", bufs=1))
-        g0_pool = ctx.enter_context(tc.tile_pool(name="g0p", bufs=2))
+        g0_pool = ctx.enter_context(tc.tile_pool(name="g0p", bufs=1))
         g1_pool = ctx.enter_context(tc.tile_pool(name="g1p", bufs=2))
         ps_a = ctx.enter_context(tc.psum_pool(name="psa", bufs=4))
         ps_b = ctx.enter_context(tc.psum_pool(name="psb", bufs=4))
@@ -110,16 +115,26 @@ def tile_dcgrucell_pa_kernel(tc, x, h, support0, support1, out):
 
         g0s = {}
 
-        def regroup_x0(b, parts=(0, 1)):
-            if b not in g0s:
-                g0_b = g0_pool.tile([P, 2, PACK * HALF], BF16, tag="g0", name="g0_%d" % b, align_bytes=64)
-                g0s[b] = g0_b
-            g0 = g0s[b]
-            for part in parts:
-                nc.vector.tensor_copy(
-                    out=g0[:, part, :].rearrange("p (c i t) -> p c t i", i=4, t=PACK),
-                    in_=raws[b][:, part].rearrange("p t (c i) -> p c t i", i=4),
-                )
+        def regroup_x0(b, engine="dve"):
+            tag = "first" if b == 0 else "later"
+            g0 = g0_pool.tile([P, 2, PACK * HALF], BF16, tag=tag, name="g0_%d" % b, align_bytes=64)
+            for part in range(2):
+                if engine == "dve":
+                    nc.vector.tensor_copy(
+                        out=g0[:, part, :].rearrange("p (c i t) -> p c t i", i=4, t=PACK),
+                        in_=raws[b][:, part].rearrange("p t (c i) -> p c t i", i=4),
+                    )
+                else:
+                    for k in range(2):
+                        nc.gpsimd.tensor_scalar(
+                            out=g0[:, part, k * PACK * CHUNK : (k + 1) * PACK * CHUNK].rearrange("p (f t) -> p f t", t=PACK),
+                            in0=raws[b][:, part, :, k * CHUNK : (k + 1) * CHUNK].rearrange("p t f -> p f t"),
+                            scalar1=1.0,
+                            scalar2=0.0,
+                            op0=MULT,
+                            op1=ADD,
+                        )
+            g0s[b] = g0
 
         def quant_x0(b, parts=(0, 2)):
             p0, p1 = parts
@@ -168,13 +183,30 @@ def tile_dcgrucell_pa_kernel(tc, x, h, support0, support1, out):
             c0 = FEAT + s * BOTH
             g1 = g1_pool.tile([P, PACK * FEAT], BF16, tag="g1", name="g1_%d" % u, align_bytes=64)
 
-            for g in range(PACK):
-                nc.scalar.copy(
-                    out=g1[:, g * PACK * CHUNK : (g + 1) * PACK * CHUNK].rearrange("p (f m) -> p f m", m=PACK),
-                    in_=a_banks[(u, g)][:].rearrange("p m f -> p f m"),
-                )
-            for g in range(PACK):
-                nc.scalar.copy(out=rows[b][:, :, c0 + g * CHUNK : c0 + (g + 1) * CHUNK], in_=a_banks[(u, g)][:])
+            def regrouped(g):
+                return g1[:, g * PACK * CHUNK : (g + 1) * PACK * CHUNK].rearrange("p (f m) -> p f m", m=PACK)
+
+            def staged(g):
+                return rows[b][:, :, c0 + g * CHUNK : c0 + (g + 1) * CHUNK]
+
+            n = vector_chunks(u)
+            for g in range(n):
+                nc.scalar.copy(out=staged(g), in_=a_banks[(u, g)][:])
+                if REGROUP == "pool":
+                    nc.gpsimd.tensor_scalar(
+                        out=regrouped(g),
+                        in0=staged(g).rearrange("p m f -> p f m"),
+                        scalar1=1.0,
+                        scalar2=0.0,
+                        op0=MULT,
+                        op1=ADD,
+                    )
+                else:
+                    nc.vector.tensor_copy(out=regrouped(g), in_=staged(g).rearrange("p m f -> p f m"))
+            for g in range(n, PACK):
+                nc.scalar.copy(out=regrouped(g), in_=a_banks[(u, g)][:].rearrange("p m f -> p f m"))
+            for g in range(n, PACK):
+                nc.scalar.copy(out=staged(g), in_=a_banks[(u, g)][:])
             g1s[u] = g1
 
         def quant_x1(u):
@@ -231,7 +263,7 @@ def tile_dcgrucell_pa_kernel(tc, x, h, support0, support1, out):
             load_x0(b)
 
         transpose_s(0)
-        transpose_s(1, (0,))
+        transpose_s(1)
         s_out(0, 0, nc.scalar.copy)
         s_out(0, 1, nc.scalar.copy)
         regroup_x0(0)
@@ -241,36 +273,25 @@ def tile_dcgrucell_pa_kernel(tc, x, h, support0, support1, out):
         quant_x0(0, (1, 2))
         cast_x0(0, 1, "act", store=True)
         step1(0, range(PACK))
-        transpose_s(1, (1,))
-        s_out(1, 0, nc.vector.tensor_copy)
+        s_out(1, 0, nc.scalar.copy)
+        s_out(1, 1, nc.scalar.copy)
         cast_x0(1, 0, "dve", store=True)
         cast_x0(1, 1, "dve", store=True)
+        quant_s(1)
         cast_x0(2, 0, "dve", store=True)
-        cast_x0(2, 1, "dve", store=True)
 
         for u in range(UNITS):
             drain1(u)
+            quant_x1(u)
+            if u + 1 < UNITS:
+                step1(u + 1, range(PACK))
+            step2(u, range(PACK))
             if u == 0:
-                quant_x1(u)
-                s_out(1, 1, nc.vector.tensor_copy)
-                quant_s(1)
-            if u >= 1:
-                quant_x1(u)
-                for banks, tiles in (([0, 1], [0]), ([2], [1]), ([3], [2, 3])):
-                    if u + 1 < UNITS:
-                        step1(u + 1, banks)
-                    step2(u, tiles)
-            else:
-                if u + 1 < UNITS:
-                    step1(u + 1, range(PACK))
-                if u > 0:
-                    quant_x1(u)
-                step2(u, range(PACK))
-            if u == 0:
-                regroup_x0(1)
-                quant_x0(1)
+                cast_x0(2, 1, "dve", store=True)
                 cast_x0(3, 0, "dve", store=True)
+                regroup_x0(1)
                 cast_x0(3, 1, "dve", store=True)
+                quant_x0(1)
             elif u == 1:
                 regroup_x0(2)
             elif u == 2:

@@ -25,41 +25,31 @@ OUT_COLS = 2560
 
 FLOPS = 2 * NSUP * 2 * BATCH * NODES * NODES * FEAT
 
-MANUAL = True
-
 X1 = FEAT
 BOTH = 2 * FEAT
-UNIT0 = FEAT
-UNIT1 = FEAT + BOTH
+FIRST = FEAT
+SECOND = FEAT + BOTH
 
 STORES = {
-    (0, 1): [(0, 2, UNIT0, BOTH)],
-    (0, 3): [(2, 2, UNIT0, BOTH)],
-    (1, 1): [(0, 2, UNIT1, BOTH)],
-    (1, 3): [(2, 2, UNIT1, BOTH)],
-    (2, 1): [(0, 2, UNIT0, BOTH)],
-    (3, 1): [(0, 2, UNIT1, BOTH)],
-    (3, 3): [(2, 2, UNIT0, 2 * BOTH)],
-    (5, 1): [(0, 2, UNIT0, 2 * BOTH)],
-    (5, 3): [(2, 2, UNIT0, 2 * BOTH)],
-    (7, 1): [(0, 2, UNIT0, 2 * BOTH)],
-    (7, 3): [(2, 2, UNIT0, 2 * BOTH)],
+    (0, 1): (0, 2, FIRST, BOTH),
+    (0, 3): (2, 2, FIRST, BOTH),
+    (1, 1): (0, 2, SECOND, BOTH),
+    (1, 3): (2, 2, SECOND, BOTH),
+    (2, 1): (0, 2, FIRST, BOTH),
+    (3, 1): (0, 2, SECOND, BOTH),
+    (3, 3): (2, 2, FIRST, 2 * BOTH),
+    (5, 1): (0, 2, FIRST, 2 * BOTH),
+    (5, 3): (2, 2, FIRST, 2 * BOTH),
+    (7, 3): (0, 4, FIRST, 2 * BOTH),
 }
-REGROUP = "pool"
-
-
-def vector_chunks(u):
-    return 1 if u >= 1 else 0
 
 
 def tile_dcgrucell_pa_kernel(tc, x, h, support0, support1, out):
     nc = tc.nc
     supports = (support0, support1)
     with ExitStack() as ctx:
-        if MANUAL:
-            ctx.enter_context(tc.manual_schedule())
+        ctx.enter_context(tc.manual_schedule())
         keep = ctx.enter_context(tc.tile_pool(name="keep", bufs=1))
-        g0_pool = ctx.enter_context(tc.tile_pool(name="g0p", bufs=1))
         g1_pool = ctx.enter_context(tc.tile_pool(name="g1p", bufs=2))
         ps_a = ctx.enter_context(tc.psum_pool(name="psa", bufs=4))
         ps_b = ctx.enter_context(tc.psum_pool(name="psb", bufs=4))
@@ -67,94 +57,76 @@ def tile_dcgrucell_pa_kernel(tc, x, h, support0, support1, out):
         ident = keep.tile([P, P], F32, name="ident")
         make_identity(nc, ident[:])
 
-        raws = []
-        rows = []
-        for b in range(BATCH):
-            raw_b = keep.tile([P, 2, PACK, HALF], BF16, name="raw%d" % b)
-            raws.append(raw_b)
-            rows_b = keep.tile([P, PACK, OUT_COLS], F32, name="rows%d" % b)
-            rows.append(rows_b)
-        s_raws = []
-        s_grps = []
-        for s in range(NSUP):
-            s_raw = keep.tile([P, PACK * NODES], BF16, name="sraw%d" % s)
-            s_raws.append(s_raw)
-            s_grp = keep.tile([P, PACK * NODES], BF16, name="sgrp%d" % s, align_bytes=64)
-            s_grps.append(s_grp)
+        raw = keep.tile([P, BATCH, 2, PACK, HALF], BF16, name="raw")
+        rows = keep.tile([P, BATCH, PACK, OUT_COLS], F32, name="rows")
+        s_raw = keep.tile([P, NSUP, PACK * NODES], BF16, name="sraw")
+        s_grp = keep.tile([P, NSUP, PACK * NODES], BF16, name="sgrp", align_bytes=64)
         s_codes = keep.tile([P, NSUP, NODES], U32, name="scodes", align_bytes=64)
         s_scales = keep.tile([P, NSUP, NODES], U8, name="sscales", align_bytes=64)
+        x0_grp = keep.tile([P, BATCH, 2, PACK * HALF], BF16, name="x0grp", align_bytes=64)
         x0_codes = keep.tile([P, BATCH, FEAT], U32, name="x0codes", align_bytes=64)
         x0_scales = keep.tile([P, BATCH, FEAT], U8, name="x0scales", align_bytes=64)
 
         out_views = [out[b].rearrange("(p m) c -> p m c", m=PACK) for b in range(BATCH)]
 
-        def load_x0(b):
-            nc.sync.dma_start(out=raws[b][:, 0], in_=x[b].rearrange("(p m) f -> p m f", m=PACK))
-            nc.sync.dma_start(out=raws[b][:, 1], in_=h[b].rearrange("(p m) f -> p m f", m=PACK))
+        def load_x0(b, n=1):
+            for part, src in enumerate((x, h)):
+                nc.sync.dma_start(
+                    out=raw[:, b : b + n, part].rearrange("p b m f -> p b (m f)"),
+                    in_=src[b : b + n].rearrange("b (p m) f -> p b (m f)", m=PACK),
+                )
 
         def load_s(s):
-            nc.sync.dma_start(out=s_raws[s][:], in_=supports[s].rearrange("(c m) j -> c (m j)", m=PACK))
+            nc.sync.dma_start(out=s_raw[:, s, :], in_=supports[s].rearrange("(c m) j -> c (m j)", m=PACK))
 
         t_banks = {}
 
-        def transpose_s(s, halves=(0, 1)):
-            words = s_raws[s][:].bitcast(F32).rearrange("c (m w u) -> c m u w", m=PACK, u=2)
-            for k in halves:
+        def transpose_s(s):
+            words = s_raw[:, s, :].bitcast(F32).rearrange("c (m w u) -> c m u w", m=PACK, u=2)
+            for k in range(2):
                 tp = ps_b.tile([P, 2, 2, P], F32, tag="b", name="tp%d%d" % (s, k))
                 for mm in range(2):
                     for u in range(2):
                         nc.tensor.transpose(tp[:, mm, u, :], words[:, 2 * k + mm, u, :], ident[:])
                 t_banks[(s, k)] = tp
 
-        def s_out(s, k, engine_copy):
-            dst = s_grps[s][:].bitcast(F32).rearrange("p (m c u) -> p m c u", m=PACK, u=2)
-            engine_copy(out=dst[:, 2 * k : 2 * k + 2], in_=t_banks[(s, k)][:].rearrange("p m u c -> p m c u"))
+        def s_out(s):
+            dst = s_grp[:, s, :].bitcast(F32).rearrange("p (m c u) -> p m c u", m=PACK, u=2)
+            for k in range(2):
+                nc.scalar.copy(out=dst[:, 2 * k : 2 * k + 2], in_=t_banks[(s, k)][:].rearrange("p m u c -> p m c u"))
 
         def quant_s(s):
-            nc.vector.quantize_mx(out=s_codes[:, s, :].bitcast(FP8X4), scales=s_scales[:, s, :], in_=s_grps[s][:])
+            nc.vector.quantize_mx(out=s_codes[:, s, :].bitcast(FP8X4), scales=s_scales[:, s, :], in_=s_grp[:, s, :])
 
-        g0s = {}
+        def regroup_x0(b, parts=range(2)):
+            for part in parts:
+                nc.vector.tensor_copy(
+                    out=x0_grp[:, b, part, :].rearrange("p (c i t) -> p c t i", i=4, t=PACK),
+                    in_=raw[:, b, part].rearrange("p t (c i) -> p c t i", i=4),
+                )
 
-        def regroup_x0(b, engine="dve"):
-            tag = "first" if b == 0 else "later"
-            g0 = g0_pool.tile([P, 2, PACK * HALF], BF16, tag=tag, name="g0_%d" % b, align_bytes=64)
-            for part in range(2):
-                if engine == "dve":
-                    nc.vector.tensor_copy(
-                        out=g0[:, part, :].rearrange("p (c i t) -> p c t i", i=4, t=PACK),
-                        in_=raws[b][:, part].rearrange("p t (c i) -> p c t i", i=4),
-                    )
-                else:
-                    for k in range(2):
-                        nc.gpsimd.tensor_scalar(
-                            out=g0[:, part, k * PACK * CHUNK : (k + 1) * PACK * CHUNK].rearrange("p (f t) -> p f t", t=PACK),
-                            in0=raws[b][:, part, :, k * CHUNK : (k + 1) * CHUNK].rearrange("p t f -> p f t"),
-                            scalar1=1.0,
-                            scalar2=0.0,
-                            op0=MULT,
-                            op1=ADD,
-                        )
-            g0s[b] = g0
-
-        def quant_x0(b, parts=(0, 2)):
-            p0, p1 = parts
+        def quant_x0(b, p0=0, p1=2):
             cols = slice(p0 * HALF, p1 * HALF)
             nc.vector.quantize_mx(
                 out=x0_codes[:, b, cols].bitcast(FP8X4),
                 scales=x0_scales[:, b, cols],
-                in_=g0s[b][:, p0:p1, :].rearrange("p s w -> p (s w)"),
+                in_=x0_grp[:, b, p0:p1, :].rearrange("p s w -> p (s w)"),
             )
 
-        def cast_x0(b, half, engine, store=False):
-            st0 = rows[b]
-            tiles = slice(2 * half, 2 * half + 2)
-            copy = nc.scalar.copy if engine == "act" else nc.vector.tensor_copy
+        def store(b, t0, nt, col, ncol):
+            tiles, cols = slice(t0, t0 + nt), slice(col, col + ncol)
+            nc.sync.dma_start(out=out_views[b][:, tiles, cols], in_=rows[:, b, tiles, cols])
+
+        def cast_x0(b, t0, nt, copy):
+            tiles = slice(t0, t0 + nt)
             copy(
-                out=st0[:, tiles, 0:FEAT].rearrange("p m (s f) -> p m s f", s=2),
-                in_=raws[b][:, :, tiles, :].rearrange("p s m f -> p m s f"),
+                out=rows[:, b, tiles, 0:FEAT].rearrange("p m (s f) -> p m s f", s=2),
+                in_=raw[:, b, :, tiles, :].rearrange("p s m f -> p m s f"),
             )
-            if store:
-                nc.sync.dma_start(out=out_views[b][:, tiles, 0:FEAT], in_=st0[:, tiles, 0:FEAT])
+
+        def x0_out(b, t0, nt, copy=nc.vector.tensor_copy):
+            cast_x0(b, t0, nt, copy)
+            store(b, t0, nt, 0, FEAT)
 
         a_banks = {}
         g1s = {}
@@ -166,11 +138,11 @@ def tile_dcgrucell_pa_kernel(tc, x, h, support0, support1, out):
                 bank = ps_a.tile([P, PACK, CHUNK], F32, tag="a", name="a%d_%d" % (u, g))
                 cols = slice(g * CHUNK, (g + 1) * CHUNK)
                 for m in range(PACK):
-                    rows = slice(m * P, (m + 1) * P)
+                    nodes = slice(m * P, (m + 1) * P)
                     nc.tensor.matmul_mx(
                         out=bank[:, m, :],
-                        lhsT=s_codes[:, s, rows].bitcast(FP8X4),
-                        lhsT_scale=s_scales[:, s, rows],
+                        lhsT=s_codes[:, s, nodes].bitcast(FP8X4),
+                        lhsT_scale=s_scales[:, s, nodes],
                         rhs=x0_codes[:, b, cols].bitcast(FP8X4),
                         rhs_scale=x0_scales[:, b, cols],
                         start=True,
@@ -183,29 +155,26 @@ def tile_dcgrucell_pa_kernel(tc, x, h, support0, support1, out):
             c0 = FEAT + s * BOTH
             g1 = g1_pool.tile([P, PACK * FEAT], BF16, tag="g1", name="g1_%d" % u, align_bytes=64)
 
-            def regrouped(g):
+            def grouped(g):
                 return g1[:, g * PACK * CHUNK : (g + 1) * PACK * CHUNK].rearrange("p (f m) -> p f m", m=PACK)
 
             def staged(g):
-                return rows[b][:, :, c0 + g * CHUNK : c0 + (g + 1) * CHUNK]
+                return rows[:, b, :, c0 + g * CHUNK : c0 + (g + 1) * CHUNK]
 
-            n = vector_chunks(u)
-            for g in range(n):
+            on_pool = 0 if u == 0 else 1
+            for g in range(on_pool):
                 nc.scalar.copy(out=staged(g), in_=a_banks[(u, g)][:])
-                if REGROUP == "pool":
-                    nc.gpsimd.tensor_scalar(
-                        out=regrouped(g),
-                        in0=staged(g).rearrange("p m f -> p f m"),
-                        scalar1=1.0,
-                        scalar2=0.0,
-                        op0=MULT,
-                        op1=ADD,
-                    )
-                else:
-                    nc.vector.tensor_copy(out=regrouped(g), in_=staged(g).rearrange("p m f -> p f m"))
-            for g in range(n, PACK):
-                nc.scalar.copy(out=regrouped(g), in_=a_banks[(u, g)][:].rearrange("p m f -> p f m"))
-            for g in range(n, PACK):
+                nc.gpsimd.tensor_scalar(
+                    out=grouped(g),
+                    in0=staged(g).rearrange("p m f -> p f m"),
+                    scalar1=1.0,
+                    scalar2=0.0,
+                    op0=MULT,
+                    op1=ADD,
+                )
+            for g in range(on_pool, PACK):
+                nc.scalar.copy(out=grouped(g), in_=a_banks[(u, g)][:].rearrange("p m f -> p f m"))
+            for g in range(on_pool, PACK):
                 nc.scalar.copy(out=staged(g), in_=a_banks[(u, g)][:])
             g1s[u] = g1
 
@@ -218,15 +187,15 @@ def tile_dcgrucell_pa_kernel(tc, x, h, support0, support1, out):
         b_banks = {}
 
         def step2(u, tiles):
-            b, s = divmod(u, NSUP)
+            s = u % NSUP
             codes, scales = x1q[u]
             for m in tiles:
-                rows = slice(m * P, (m + 1) * P)
+                nodes = slice(m * P, (m + 1) * P)
                 bank = ps_b.tile([P, 2, HALF], F32, tag="b", name="b%d_%d" % (u, m))
                 nc.tensor.matmul_mx(
                     out=bank[:].rearrange("p s f -> p (s f)"),
-                    lhsT=s_codes[:, s, rows].bitcast(FP8X4),
-                    lhsT_scale=s_scales[:, s, rows],
+                    lhsT=s_codes[:, s, nodes].bitcast(FP8X4),
+                    lhsT_scale=s_scales[:, s, nodes],
                     rhs=codes[:].bitcast(FP8X4),
                     rhs_scale=scales[:],
                     start=True,
@@ -234,23 +203,20 @@ def tile_dcgrucell_pa_kernel(tc, x, h, support0, support1, out):
                 )
                 b_banks[(u, m)] = bank
 
-        def drain2(u):
+        def drain2(u, tiles=range(PACK)):
             b, s = divmod(u, NSUP)
             c0 = FEAT + s * BOTH + X1
-            for m in range(PACK):
+            for m in tiles:
                 nc.vector.scalar_tensor_tensor(
-                    out=rows[b][:, m, c0 : c0 + FEAT].rearrange("p (s f) -> p s f", s=2),
+                    out=rows[:, b, m, c0 : c0 + FEAT].rearrange("p (s f) -> p s f", s=2),
                     in0=b_banks[(u, m)][:],
                     scalar=2.0,
-                    in1=raws[b][:, :, m, :],
+                    in1=raw[:, b, :, m, :],
                     op0=MULT,
                     op1=SUBTRACT,
                 )
-                for t0, nt, col, ncol in STORES.get((u, m), []):
-                    nc.sync.dma_start(
-                        out=out_views[b][:, t0 : t0 + nt, col : col + ncol],
-                        in_=rows[b][:, t0 : t0 + nt, col : col + ncol],
-                    )
+                if (u, m) in STORES:
+                    store(b, *STORES[(u, m)])
 
         warm = keep.tile([P, 2], F32, name="warm")
         nc.vector.memset(warm[:], 0.0)
@@ -259,26 +225,24 @@ def tile_dcgrucell_pa_kernel(tc, x, h, support0, support1, out):
         load_s(0)
         load_x0(0)
         load_s(1)
-        for b in range(1, BATCH):
-            load_x0(b)
+        load_x0(1)
+        load_x0(2, 2)
 
         transpose_s(0)
         transpose_s(1)
-        s_out(0, 0, nc.scalar.copy)
-        s_out(0, 1, nc.scalar.copy)
-        regroup_x0(0)
-        quant_x0(0, (0, 1))
-        cast_x0(0, 0, "dve", store=True)
+        s_out(0)
+        regroup_x0(0, (0,))
+        x0_out(0, 0, 2)
+        quant_x0(0, 0, 1)
         quant_s(0)
-        quant_x0(0, (1, 2))
-        cast_x0(0, 1, "act", store=True)
+        regroup_x0(0, (1,))
+        quant_x0(0, 1, 2)
+        x0_out(0, 2, 2, nc.scalar.copy)
         step1(0, range(PACK))
-        s_out(1, 0, nc.scalar.copy)
-        s_out(1, 1, nc.scalar.copy)
-        cast_x0(1, 0, "dve", store=True)
-        cast_x0(1, 1, "dve", store=True)
+        s_out(1)
+        x0_out(1, 0, 4)
         quant_s(1)
-        cast_x0(2, 0, "dve", store=True)
+        x0_out(2, 0, 2)
 
         for u in range(UNITS):
             drain1(u)
@@ -287,17 +251,19 @@ def tile_dcgrucell_pa_kernel(tc, x, h, support0, support1, out):
                 step1(u + 1, range(PACK))
             step2(u, range(PACK))
             if u == 0:
-                cast_x0(2, 1, "dve", store=True)
-                cast_x0(3, 0, "dve", store=True)
+                x0_out(2, 2, 2)
+                x0_out(3, 0, 4)
                 regroup_x0(1)
-                cast_x0(3, 1, "dve", store=True)
+                drain2(0, range(2))
                 quant_x0(1)
-            elif u == 1:
+                drain2(0, range(2, PACK))
+            if u == 1:
                 regroup_x0(2)
-            elif u == 2:
+            if u == 2:
                 quant_x0(2)
-            elif u == 3:
+            if u == 3:
                 regroup_x0(3)
-            elif u == 4:
+            if u == 4:
                 quant_x0(3)
-            drain2(u)
+            if u > 0:
+                drain2(u)

from contextlib import ExitStack

import concourse.mybir as mybir
from concourse.masks import make_identity

F32 = mybir.dt.float32
BF16 = mybir.dt.bfloat16
U32 = mybir.dt.uint32
U8 = mybir.dt.uint8
FP8X4 = mybir.dt.float8_e4m3fn_x4
MULT = mybir.AluOpType.mult
SUBTRACT = mybir.AluOpType.subtract
ADD = mybir.AluOpType.add

P = 128
PACK = 4
BATCH = 4
NODES = 512
HALF = 256
FEAT = 512
NSUP = 2
UNITS = BATCH * NSUP
CHUNK = 128
OUT_COLS = 2560

FLOPS = 2 * NSUP * 2 * BATCH * NODES * NODES * FEAT

X1 = FEAT
BOTH = 2 * FEAT
FIRST = FEAT
SECOND = FEAT + BOTH

STORES = {
    (0, 1): (0, 2, FIRST, BOTH),
    (0, 3): (2, 2, FIRST, BOTH),
    (1, 1): (0, 2, SECOND, BOTH),
    (1, 3): (2, 2, SECOND, BOTH),
    (2, 1): (0, 2, FIRST, BOTH),
    (3, 1): (0, 2, SECOND, BOTH),
    (3, 3): (2, 2, FIRST, 2 * BOTH),
    (5, 1): (0, 2, FIRST, 2 * BOTH),
    (5, 3): (2, 2, FIRST, 2 * BOTH),
    (7, 3): (0, 4, FIRST, 2 * BOTH),
}


def tile_dcgrucell_pa_kernel(tc, x, h, support0, support1, out):
    nc = tc.nc
    supports = (support0, support1)
    with ExitStack() as ctx:
        ctx.enter_context(tc.manual_schedule())
        keep = ctx.enter_context(tc.tile_pool(name="keep", bufs=1))
        g1_pool = ctx.enter_context(tc.tile_pool(name="g1p", bufs=2))
        ps_a = ctx.enter_context(tc.psum_pool(name="psa", bufs=4))
        ps_b = ctx.enter_context(tc.psum_pool(name="psb", bufs=4))

        ident = keep.tile([P, P], F32, name="ident")
        make_identity(nc, ident[:])

        raw = keep.tile([P, BATCH, 2, PACK, HALF], BF16, name="raw")
        rows = keep.tile([P, BATCH, PACK, OUT_COLS], F32, name="rows")
        s_raw = keep.tile([P, NSUP, PACK * NODES], BF16, name="sraw")
        s_grp = keep.tile([P, NSUP, PACK * NODES], BF16, name="sgrp", align_bytes=64)
        s_codes = keep.tile([P, NSUP, NODES], U32, name="scodes", align_bytes=64)
        s_scales = keep.tile([P, NSUP, NODES], U8, name="sscales", align_bytes=64)
        x0_grp = keep.tile([P, BATCH, 2, PACK * HALF], BF16, name="x0grp", align_bytes=64)
        x0_codes = keep.tile([P, BATCH, FEAT], U32, name="x0codes", align_bytes=64)
        x0_scales = keep.tile([P, BATCH, FEAT], U8, name="x0scales", align_bytes=64)

        out_views = [out[b].rearrange("(p m) c -> p m c", m=PACK) for b in range(BATCH)]

        def load_x0(b, n=1):
            for part, src in enumerate((x, h)):
                nc.sync.dma_start(
                    out=raw[:, b : b + n, part].rearrange("p b m f -> p b (m f)"),
                    in_=src[b : b + n].rearrange("b (p m) f -> p b (m f)", m=PACK),
                )

        def load_s(s):
            nc.sync.dma_start(out=s_raw[:, s, :], in_=supports[s].rearrange("(c m) j -> c (m j)", m=PACK))

        t_banks = {}

        def transpose_s(s):
            words = s_raw[:, s, :].bitcast(F32).rearrange("c (m w u) -> c m u w", m=PACK, u=2)
            for k in range(2):
                tp = ps_b.tile([P, 2, 2, P], F32, tag="b", name="tp%d%d" % (s, k))
                for mm in range(2):
                    for u in range(2):
                        nc.tensor.transpose(tp[:, mm, u, :], words[:, 2 * k + mm, u, :], ident[:])
                t_banks[(s, k)] = tp

        def s_out(s):
            dst = s_grp[:, s, :].bitcast(F32).rearrange("p (m c u) -> p m c u", m=PACK, u=2)
            for k in range(2):
                nc.scalar.copy(out=dst[:, 2 * k : 2 * k + 2], in_=t_banks[(s, k)][:].rearrange("p m u c -> p m c u"))

        def quant_s(s):
            nc.vector.quantize_mx(out=s_codes[:, s, :].bitcast(FP8X4), scales=s_scales[:, s, :], in_=s_grp[:, s, :])

        def regroup_x0(b, parts=range(2)):
            for part in parts:
                nc.vector.tensor_copy(
                    out=x0_grp[:, b, part, :].rearrange("p (c i t) -> p c t i", i=4, t=PACK),
                    in_=raw[:, b, part].rearrange("p t (c i) -> p c t i", i=4),
                )

        def quant_x0(b, p0=0, p1=2):
            cols = slice(p0 * HALF, p1 * HALF)
            nc.vector.quantize_mx(
                out=x0_codes[:, b, cols].bitcast(FP8X4),
                scales=x0_scales[:, b, cols],
                in_=x0_grp[:, b, p0:p1, :].rearrange("p s w -> p (s w)"),
            )

        def store(b, t0, nt, col, ncol):
            tiles, cols = slice(t0, t0 + nt), slice(col, col + ncol)
            nc.sync.dma_start(out=out_views[b][:, tiles, cols], in_=rows[:, b, tiles, cols])

        def cast_x0(b, t0, nt, copy):
            tiles = slice(t0, t0 + nt)
            copy(
                out=rows[:, b, tiles, 0:FEAT].rearrange("p m (s f) -> p m s f", s=2),
                in_=raw[:, b, :, tiles, :].rearrange("p s m f -> p m s f"),
            )

        def x0_out(b, t0, nt, copy=nc.vector.tensor_copy):
            cast_x0(b, t0, nt, copy)
            store(b, t0, nt, 0, FEAT)

        a_banks = {}
        g1s = {}
        x1q = {}

        def step1(u, chunks):
            b, s = divmod(u, NSUP)
            for g in chunks:
                bank = ps_a.tile([P, PACK, CHUNK], F32, tag="a", name="a%d_%d" % (u, g))
                cols = slice(g * CHUNK, (g + 1) * CHUNK)
                for m in range(PACK):
                    nodes = slice(m * P, (m + 1) * P)
                    nc.tensor.matmul_mx(
                        out=bank[:, m, :],
                        lhsT=s_codes[:, s, nodes].bitcast(FP8X4),
                        lhsT_scale=s_scales[:, s, nodes],
                        rhs=x0_codes[:, b, cols].bitcast(FP8X4),
                        rhs_scale=x0_scales[:, b, cols],
                        start=True,
                        stop=True,
                    )
                a_banks[(u, g)] = bank

        def drain1(u):
            b, s = divmod(u, NSUP)
            c0 = FEAT + s * BOTH
            g1 = g1_pool.tile([P, PACK * FEAT], BF16, tag="g1", name="g1_%d" % u, align_bytes=64)

            def grouped(g):
                return g1[:, g * PACK * CHUNK : (g + 1) * PACK * CHUNK].rearrange("p (f m) -> p f m", m=PACK)

            def staged(g):
                return rows[:, b, :, c0 + g * CHUNK : c0 + (g + 1) * CHUNK]

            on_pool = 0 if u == 0 else 1
            for g in range(on_pool):
                nc.scalar.copy(out=staged(g), in_=a_banks[(u, g)][:])
                nc.gpsimd.tensor_scalar(
                    out=grouped(g),
                    in0=staged(g).rearrange("p m f -> p f m"),
                    scalar1=1.0,
                    scalar2=0.0,
                    op0=MULT,
                    op1=ADD,
                )
            for g in range(on_pool, PACK):
                nc.scalar.copy(out=grouped(g), in_=a_banks[(u, g)][:].rearrange("p m f -> p f m"))
            for g in range(on_pool, PACK):
                nc.scalar.copy(out=staged(g), in_=a_banks[(u, g)][:])
            g1s[u] = g1

        def quant_x1(u):
            codes = g1_pool.tile([P, FEAT], U32, tag="x1c", name="x1c_%d" % u, align_bytes=64)
            scales = g1_pool.tile([P, FEAT], U8, tag="x1s", name="x1s_%d" % u, align_bytes=64)
            nc.vector.quantize_mx(out=codes[:].bitcast(FP8X4), scales=scales[:], in_=g1s[u][:])
            x1q[u] = (codes, scales)

        b_banks = {}

        def step2(u, tiles):
            s = u % NSUP
            codes, scales = x1q[u]
            for m in tiles:
                nodes = slice(m * P, (m + 1) * P)
                bank = ps_b.tile([P, 2, HALF], F32, tag="b", name="b%d_%d" % (u, m))
                nc.tensor.matmul_mx(
                    out=bank[:].rearrange("p s f -> p (s f)"),
                    lhsT=s_codes[:, s, nodes].bitcast(FP8X4),
                    lhsT_scale=s_scales[:, s, nodes],
                    rhs=codes[:].bitcast(FP8X4),
                    rhs_scale=scales[:],
                    start=True,
                    stop=True,
                )
                b_banks[(u, m)] = bank

        def drain2(u, tiles=range(PACK)):
            b, s = divmod(u, NSUP)
            c0 = FEAT + s * BOTH + X1
            for m in tiles:
                nc.vector.scalar_tensor_tensor(
                    out=rows[:, b, m, c0 : c0 + FEAT].rearrange("p (s f) -> p s f", s=2),
                    in0=b_banks[(u, m)][:],
                    scalar=2.0,
                    in1=raw[:, b, :, m, :],
                    op0=MULT,
                    op1=SUBTRACT,
                )
                if (u, m) in STORES:
                    store(b, *STORES[(u, m)])

        warm = keep.tile([P, 2], F32, name="warm")
        nc.vector.memset(warm[:], 0.0)
        nc.scalar.copy(out=warm[:, 1:2], in_=warm[:, 0:1])

        load_s(0)
        load_x0(0)
        load_s(1)
        load_x0(1)
        load_x0(2, 2)

        transpose_s(0)
        transpose_s(1)
        s_out(0)
        regroup_x0(0, (0,))
        x0_out(0, 0, 2)
        quant_x0(0, 0, 1)
        quant_s(0)
        regroup_x0(0, (1,))
        quant_x0(0, 1, 2)
        x0_out(0, 2, 2, nc.scalar.copy)
        step1(0, range(PACK))
        s_out(1)
        x0_out(1, 0, 4)
        quant_s(1)
        x0_out(2, 0, 2)

        for u in range(UNITS):
            drain1(u)
            quant_x1(u)
            if u + 1 < UNITS:
                step1(u + 1, range(PACK))
            step2(u, range(PACK))
            if u == 0:
                x0_out(2, 2, 2)
                x0_out(3, 0, 4)
                regroup_x0(1)
                drain2(0, range(2))
                quant_x0(1)
                drain2(0, range(2, PACK))
            if u == 1:
                regroup_x0(2)
            if u == 2:
                quant_x0(2)
            if u == 3:
                regroup_x0(3)
            if u == 4:
                quant_x0(3)
            if u > 0:
                drain2(u)
